import numpy as np
import ml_dtypes


def mxq(x, axis, fmt="e4m3"):
    dtype, down = {"e4m3": (ml_dtypes.float8_e4m3fn, 7), "e5m2": (ml_dtypes.float8_e5m2, 14)}[fmt]
    v = np.moveaxis(np.asarray(x, np.float32).astype(ml_dtypes.bfloat16).astype(np.float64), axis, -1)
    blocks = v.reshape(v.shape[:-1] + (-1, 32))
    amax = np.abs(blocks).max(-1, keepdims=True)
    byte = np.maximum(np.where(amax > 0, np.frexp(amax)[1] - 1 + 127, 0) - down, 1)
    scale = np.exp2(byte - 127.0)
    codes = (blocks / scale).astype(np.float32).astype(dtype).astype(np.float64)
    return np.moveaxis((codes * scale).reshape(v.shape), -1, axis)


WIDE = False


def mx_kscale(k):
    if not WIDE:
        return np.ones(k)
    levels = np.array([10, -10, 5, -5, 0])
    a = np.random.permutation(np.resize(levels, k // 512 * 4)).reshape(k // 512, 4)
    idx = np.arange(k)
    return np.exp2(a[idx // 512, idx % 128 // 32])


BF16 = ml_dtypes.bfloat16


def bf(x):
    return np.asarray(x, np.float32).astype(BF16)


def f64(x):
    return np.asarray(x).astype(np.float64)


B, M, N, P = 4, 1024, 2048, 128
EPS = 1e-05


def normalize(v, axes, gamma, beta):
    mean = v.mean(axis=axes, keepdims=True)
    std = np.sqrt(v.var(axis=axes, keepdims=True, ddof=1))
    return gamma * ((v - mean) / (std + EPS)) + beta


def setup_inputs():
    s = mx_kscale(M)
    return {"x": bf(np.random.standard_normal((B, M, N)) * s[:, None]),
            "permuted_xj_y": bf(np.random.standard_normal((M, P)) * 0.5 / np.sqrt(M) / s[:, None]),
            "permuted_xi_y": bf(np.random.standard_normal((N, P)) * 2.0 / np.sqrt(N)),
            "gamma_p_sum": bf(1.0 + 0.1 * np.random.standard_normal(P)),
            "gamma_p": bf(1.0 + 0.1 * np.random.standard_normal((P, P))),
            "beta_p_sum": bf(0.1 * np.random.standard_normal(P)),
            "beta_p": bf(0.1 * np.random.standard_normal((P, P)))}


def reference(x, permuted_xj_y, permuted_xi_y, gamma_p_sum, gamma_p, beta_p_sum, beta_p):
    permuted = np.swapaxes(f64(x), -1, -2)
    pyy = mxq(permuted, 2, "e4m3") @ mxq(f64(permuted_xj_y), 0, "e4m3")
    p_sum = normalize(pyy.sum(axis=-2), (-1,), f64(gamma_p_sum), f64(beta_p_sum)) + 1.0
    pyy = mxq(np.swapaxes(pyy, -1, -2), 2, "e4m3") @ mxq(f64(permuted_xi_y), 0, "e4m3")
    pyy = np.swapaxes(pyy, -1, -2)
    pyy = normalize(pyy, (-2, -1), f64(gamma_p), f64(beta_p))
    return pyy, p_sum

@@ -1,0 +1,342 @@
+from contextlib import ExitStack
+
+import concourse.mybir as mybir
+
+F32 = mybir.dt.float32
+BF16 = mybir.dt.bfloat16
+U32 = mybir.dt.uint32
+U8 = mybir.dt.uint8
+FP8X4 = mybir.dt.float8_e4m3fn_x4
+ACT = mybir.ActivationFunctionType
+ALU = mybir.AluOpType
+
+BATCH = 4
+M_ROWS = 1024
+N_COLS = 2048
+PROJ = 128
+EPS = 1e-5
+
+P = 128
+PACK = 4
+K_PASS = P * PACK
+M_PASSES = M_ROWS // K_PASS
+N_PASSES = N_COLS // K_PASS
+
+VECTOR_COLS = 272
+RUN = 4
+LOAD_PARTS = 2
+
+FLOPS = 2 * BATCH * N_COLS * M_ROWS * PROJ + 2 * BATCH * PROJ * N_COLS * PROJ
+
+
+def tile_selfprojection_pb_t_kernel(
+    tc, x, permuted_xj_y, permuted_xi_y, gamma_p_sum, gamma_p, beta_p_sum, beta_p, out_0, out_1
+):
+    nc = tc.nc
+    with ExitStack() as ctx:
+        keep = ctx.enter_context(tc.tile_pool(name="keep", bufs=1))
+        codes_pool = ctx.enter_context(tc.tile_pool(name="codes", bufs=2))
+        stage = ctx.enter_context(tc.tile_pool(name="stage", bufs=3))
+        finish = ctx.enter_context(tc.tile_pool(name="finish", bufs=2))
+        psum_y = ctx.enter_context(tc.psum_pool(name="psum_y", bufs=3))
+        psum_one = ctx.enter_context(tc.psum_pool(name="psum_one", bufs=1))
+
+        warm = keep.tile([P, 1], F32)
+        nc.vector.memset(warm[:], 1.0)
+        nc.scalar.activation(out=warm[:], in_=warm[:], func=ACT.Sqrt)
+
+        ones = keep.tile([P, P], F32)
+        nc.vector.memset(ones[:], 1.0)
+        select = keep.tile([P, BATCH, P], F32)
+        nc.vector.memset(select[:], 0.0)
+        for b in range(BATCH):
+            nc.vector.memset(select[:, b, b : b + 1], 1.0)
+
+        x_rows = {}
+
+        def load_x(b, c):
+            x_rows[b, c] = keep.tile([P, PACK, N_COLS], BF16, name="x_rows_%d_%d" % (b, c))
+            source = x[b, c * K_PASS : (c + 1) * K_PASS, :].rearrange("(p j) n -> p j n", j=PACK)
+            width = N_COLS // LOAD_PARTS
+            for part in range(LOAD_PARTS):
+                cols = slice(part * width, (part + 1) * width)
+                nc.sync.dma_start(out=x_rows[b, c][:, :, cols], in_=source[:, :, cols])
+
+        load_x(0, 0)
+        xj_rows = keep.tile([P, M_PASSES, PACK, PROJ], BF16)
+        nc.sync.dma_start(
+            out=xj_rows[:], in_=permuted_xj_y.rearrange("(c p j) w -> p c j w", p=P, j=PACK)
+        )
+        xi_rows = keep.tile([P, N_PASSES, PACK, PROJ], BF16)
+        nc.sync.dma_start(
+            out=xi_rows[:].rearrange("p g t w -> p (g t) w"),
+            in_=permuted_xi_y.rearrange("(a p) w -> p a w", p=P),
+        )
+        gamma_z = keep.tile([P, PROJ], BF16)
+        nc.sync.dma_start(out=gamma_z[:], in_=gamma_p)
+        beta_z = keep.tile([P, PROJ], BF16)
+        nc.sync.dma_start(out=beta_z[:], in_=beta_p)
+        gamma_c = keep.tile([BATCH, PROJ], BF16)
+        nc.sync.dma_start(out=gamma_c[:], in_=gamma_p_sum.partition_broadcast(BATCH))
+        beta_c = keep.tile([BATCH, PROJ], BF16)
+        nc.sync.dma_start(out=beta_c[:], in_=beta_p_sum.partition_broadcast(BATCH))
+        load_x(0, 1)
+        for b in range(1, BATCH):
+            for c in range(M_PASSES):
+                load_x(b, c)
+
+        xj_grouped = keep.tile([P, M_PASSES, PROJ, PACK], BF16, align_bytes=64)
+        xj_codes = keep.tile([P, M_PASSES, PROJ], U32, align_bytes=64)
+        xj_scales = keep.tile([P, M_PASSES, PROJ], U8, align_bytes=64)
+        xi_grouped = keep.tile([P, N_PASSES, PROJ, PACK], BF16, align_bytes=64)
+        xi_codes = keep.tile([P, N_PASSES, PROJ], U32, align_bytes=64)
+        xi_scales = keep.tile([P, N_PASSES, PROJ], U8, align_bytes=64)
+
+        beta_c_plus_1 = keep.tile([BATCH, PROJ], F32)
+
+        def prepare_small_operands():
+            half = N_PASSES // 2
+            nc.vector.tensor_copy(out=xj_grouped[:], in_=xj_rows[:].rearrange("p c j w -> p c w j"))
+            nc.scalar.copy(
+                out=xi_grouped[:, half:], in_=xi_rows[:, half:].rearrange("p g t w -> p g w t")
+            )
+            nc.vector.tensor_copy(
+                out=xi_grouped[:, :half], in_=xi_rows[:, :half].rearrange("p g t w -> p g w t")
+            )
+            nc.vector.quantize_mx(
+                out=xj_codes[:].rearrange("p c w -> p (c w)").bitcast(FP8X4),
+                scales=xj_scales[:].rearrange("p c w -> p (c w)"),
+                in_=xj_grouped[:].rearrange("p c w j -> p (c w j)"),
+            )
+            nc.vector.tensor_scalar_add(out=beta_c_plus_1[:], in0=beta_c[:], scalar1=1.0)
+            nc.vector.quantize_mx(
+                out=xi_codes[:].rearrange("p g w -> p (g w)").bitcast(FP8X4),
+                scales=xi_scales[:].rearrange("p g w -> p (g w)"),
+                in_=xi_grouped[:].rearrange("p g w t -> p (g w t)"),
+            )
+
+        pieces = [
+            (b, c, g) for b in range(BATCH) for c in range(M_PASSES) for g in range(N_PASSES)
+        ]
+
+        def piece_at(step):
+            return pieces[step] if 0 <= step < len(pieces) else None
+
+        def group_at(step):
+            piece = piece_at(step)
+            if piece is None or piece[1] != M_PASSES - 1:
+                return None
+            return piece[0], piece[2]
+
+        def batch_at(step):
+            group = group_at(step)
+            if group is None or group[1] != N_PASSES - 1:
+                return None
+            return group[0]
+
+        x_grouped_of = {}
+        x_codes_of = {}
+        x_scales_of = {}
+        y_ps_of = {}
+        y_grouped_of = {}
+        col_sum_ps_of = {}
+        z_ps_of = {}
+        z_tiles_of = {}
+        c_tiles = {}
+        c_ps = psum_one.tile([P, PROJ], F32)
+
+        def regroup_x(step):
+            piece = piece_at(step)
+            if piece is None:
+                return
+            b, c, g = piece
+            x_grouped = stage.tile([P, K_PASS, PACK], BF16, align_bytes=64)
+            x_grouped_of[piece] = x_grouped
+            rows = x_rows[b, c][:, :, g * K_PASS : (g + 1) * K_PASS]
+            source = rows.rearrange("p j (q i) -> p q j i", i=RUN)
+            target = x_grouped[:].rearrange("p (q i) j -> p q j i", i=RUN)
+            split = VECTOR_COLS // RUN
+            nc.vector.tensor_copy(out=target[:, :split], in_=source[:, :split])
+            nc.scalar.copy(out=target[:, split:], in_=source[:, split:])
+
+        def quantise_x(step):
+            piece = piece_at(step)
+            if piece is None:
+                return
+            b, c, g = piece
+            if c == 0 and g == 0:
+                x_codes_of[b] = codes_pool.tile(
+                    [P, M_PASSES, N_COLS], U32, align_bytes=64, name="x_codes", tag="x_codes"
+                )
+                x_scales_of[b] = codes_pool.tile(
+                    [P, M_PASSES, N_COLS], U8, align_bytes=64, name="x_scales", tag="x_scales"
+                )
+            cols = slice(g * K_PASS, (g + 1) * K_PASS)
+            nc.vector.quantize_mx(
+                out=x_codes_of[b][:, c, cols].bitcast(FP8X4),
+                scales=x_scales_of[b][:, c, cols],
+                in_=x_grouped_of[piece][:].rearrange("p n j -> p (n j)"),
+            )
+
+        def project_x(step):
+            group = group_at(step)
+            if group is None:
+                return
+            b, g = group
+            y_ps = psum_y.tile([P, PACK, PROJ], F32)
+            y_ps_of[group] = y_ps
+            if g == 0:
+                col_sum_ps_of[b] = psum_one.tile([P, PROJ], F32, name="col_sum_ps", tag="col_sum_ps")
+            for t in range(PACK):
+                cols = slice(g * K_PASS + t * P, g * K_PASS + (t + 1) * P)
+                for c in range(M_PASSES):
+                    operands = dict(
+                        lhsT=x_codes_of[b][:, c, cols].bitcast(FP8X4),
+                        lhsT_scale=x_scales_of[b][:, c, cols],
+                        rhs=xj_codes[:, c, :].bitcast(FP8X4),
+                        rhs_scale=xj_scales[:, c, :],
+                    )
+                    nc.tensor.matmul_mx(
+                        out=y_ps[:, t, :], start=(c == 0), stop=(c == M_PASSES - 1), **operands
+                    )
+                    nc.tensor.matmul_mx(
+                        out=col_sum_ps_of[b][:],
+                        start=(g == 0 and t == 0 and c == 0),
+                        stop=(g == N_PASSES - 1 and t == PACK - 1 and c == M_PASSES - 1),
+                        **operands,
+                    )
+
+        def round_y(step):
+            group = group_at(step)
+            if group is None:
+                return
+            y_grouped = stage.tile([P, PROJ, PACK], BF16, align_bytes=64)
+            y_grouped_of[group] = y_grouped
+            nc.scalar.copy(out=y_grouped[:], in_=y_ps_of[group][:].rearrange("p t w -> p w t"))
+
+        def add_col_sum(step):
+            b = batch_at(step)
+            if b is None:
+                return
+            col_sum = finish.tile([P, PROJ], F32)
+            nc.vector.tensor_copy(out=col_sum[:], in_=col_sum_ps_of[b][:])
+            nc.tensor.matmul(
+                out=c_ps[:], lhsT=select[:, b, :], rhs=col_sum[:],
+                start=(b == 0), stop=(b == BATCH - 1),
+            )
+
+        def contract_y(step):
+            group = group_at(step)
+            if group is None:
+                return
+            b, g = group
+            y_codes = stage.tile([P, PROJ], U32, align_bytes=64)
+            y_scales = stage.tile([P, PROJ], U8, align_bytes=64)
+            nc.vector.quantize_mx(
+                out=y_codes[:].bitcast(FP8X4),
+                scales=y_scales[:],
+                in_=y_grouped_of[group][:].rearrange("p w t -> p (w t)"),
+            )
+            if g == 0:
+                z_ps_of[b] = psum_one.tile([P, PROJ], F32, name="z_ps", tag="z_ps")
+            nc.tensor.matmul_mx(
+                out=z_ps_of[b][:],
+                lhsT=xi_codes[:, g, :].bitcast(FP8X4),
+                lhsT_scale=xi_scales[:, g, :],
+                rhs=y_codes[:].bitcast(FP8X4),
+                rhs_scale=y_scales[:],
+                start=(g == 0),
+                stop=(g == N_PASSES - 1),
+            )
+
+
+        def small_tile(what, name, rows, cols):
+            label = what + "_" + name
+            return finish.tile([rows, cols], F32, name=label, tag=label)
+
+        def sum_values(what, rows, values_ps, add_up, tiles):
+            tiles["values"] = small_tile(what, "values", rows, PROJ)
+            row_sum = small_tile(what, "row_sum", rows, 1)
+            nc.scalar.activation(
+                out=tiles["values"][:], in_=values_ps, func=ACT.Copy, accum_out=row_sum[:]
+            )
+            tiles["total"] = add_up("total", row_sum)
+
+        def centre_values(what, rows, count, gamma, add_up, tiles):
+            neg_mean = small_tile(what, "neg_mean", rows, 1)
+            nc.vector.tensor_scalar_mul(out=neg_mean[:], in0=tiles["total"][:], scalar1=-1.0 / count)
+            squares = small_tile(what, "squares", rows, PROJ)
+            row_squares = small_tile(what, "row_squares", rows, 1)
+            nc.scalar.activation(
+                out=squares[:], in_=tiles["values"][:], func=ACT.Square, bias=neg_mean[:],
+                accum_out=row_squares[:],
+            )
+            tiles["total_squares"] = add_up("total_squares", row_squares)
+            tiles["gained"] = small_tile(what, "gained", rows, PROJ)
+            nc.vector.scalar_tensor_tensor(
+                out=tiles["gained"][:], in0=tiles["values"][:], scalar=neg_mean[:], in1=gamma,
+                op0=ALU.add, op1=ALU.mult,
+            )
+
+        def scale_values(what, rows, count, beta, tiles, destination):
+            std = small_tile(what, "std", rows, 1)
+            nc.scalar.activation(
+                out=std[:], in_=tiles["total_squares"][:], func=ACT.Sqrt, scale=1.0 / (count - 1)
+            )
+            std_eps = small_tile(what, "std_eps", rows, 1)
+            nc.vector.tensor_scalar_add(out=std_eps[:], in0=std[:], scalar1=EPS)
+            inverse = small_tile(what, "inverse", rows, 1)
+            nc.vector.reciprocal(out=inverse[:], in_=std_eps[:])
+            result = small_tile(what, "result", rows, PROJ)
+            nc.vector.scalar_tensor_tensor(
+                out=result[:], in0=tiles["gained"][:], scalar=inverse[:], in1=beta,
+                op0=ALU.mult, op1=ALU.add,
+            )
+            nc.sync.dma_start(out=destination, in_=result[:])
+
+        def over_partitions(name, column):
+            total_ps = psum_one.tile([P, 1], F32, name=name, tag=name)
+            nc.tensor.matmul(out=total_ps[:], lhsT=ones[:], rhs=column[:], start=True, stop=True)
+            return total_ps
+
+        def within_partition(name, column):
+            return column
+
+        def normalise_z(step, part):
+            b = batch_at(step)
+            if b is None:
+                return
+            if part == 0:
+                z_tiles_of[b] = {}
+                sum_values("z", P, z_ps_of[b][:], over_partitions, z_tiles_of[b])
+            if part == 1:
+                centre_values("z", P, PROJ * PROJ, gamma_z[:], over_partitions, z_tiles_of[b])
+            if part == 2:
+                scale_values("z", P, PROJ * PROJ, beta_z[:], z_tiles_of[b], out_0[b])
+
+        def normalise_c(step, part):
+            if step != len(pieces) - 1:
+                return
+            if part == 0:
+                sum_values("c", BATCH, c_ps[:BATCH, :], within_partition, c_tiles)
+            if part == 1:
+                centre_values("c", BATCH, PROJ, gamma_c[:], within_partition, c_tiles)
+            if part == 2:
+                scale_values("c", BATCH, PROJ, beta_c_plus_1[:], c_tiles, out_1)
+
+        STAGES = 7
+        for step in range(len(pieces) + STAGES - 1):
+            if step == N_PASSES:
+                prepare_small_operands()
+            regroup_x(step)
+            quantise_x(step - 1)
+            project_x(step - 1)
+            round_y(step - 2)
+            add_col_sum(step - 2)
+            contract_y(step - 3)
+            normalise_c(step - 3, 0)
+            normalise_z(step - 4, 0)
+            normalise_c(step - 4, 1)
+            normalise_z(step - 5, 1)
+            normalise_c(step - 5, 2)
+            normalise_z(step - 6, 2)

@@ -37,9 +37,10 @@ def tile_selfprojection_pb_t_kernel(
         keep = ctx.enter_context(tc.tile_pool(name="keep", bufs=1))
         codes_pool = ctx.enter_context(tc.tile_pool(name="codes", bufs=2))
         stage = ctx.enter_context(tc.tile_pool(name="stage", bufs=3))
-        finish = ctx.enter_context(tc.tile_pool(name="finish", bufs=2))
+        finish = ctx.enter_context(tc.tile_pool(name="finish", bufs=BATCH))
         psum_y = ctx.enter_context(tc.psum_pool(name="psum_y", bufs=3))
         psum_one = ctx.enter_context(tc.psum_pool(name="psum_one", bufs=1))
+        ctx.enter_context(tc.manual_schedule())
 
         warm = keep.tile([P, 1], F32)
         nc.vector.memset(warm[:], 1.0)
@@ -187,23 +188,28 @@ def tile_selfprojection_pb_t_kernel(
             y_ps_of[group] = y_ps
             if g == 0:
                 col_sum_ps_of[b] = psum_one.tile([P, PROJ], F32, name="col_sum_ps", tag="col_sum_ps")
-            for t in range(PACK):
+
+            def operands(t, c):
                 cols = slice(g * K_PASS + t * P, g * K_PASS + (t + 1) * P)
+                return dict(
+                    lhsT=x_codes_of[b][:, c, cols].bitcast(FP8X4),
+                    lhsT_scale=x_scales_of[b][:, c, cols],
+                    rhs=xj_codes[:, c, :].bitcast(FP8X4),
+                    rhs_scale=xj_scales[:, c, :],
+                )
+
+            for t in range(PACK):
                 for c in range(M_PASSES):
-                    operands = dict(
-                        lhsT=x_codes_of[b][:, c, cols].bitcast(FP8X4),
-                        lhsT_scale=x_scales_of[b][:, c, cols],
-                        rhs=xj_codes[:, c, :].bitcast(FP8X4),
-                        rhs_scale=xj_scales[:, c, :],
-                    )
                     nc.tensor.matmul_mx(
-                        out=y_ps[:, t, :], start=(c == 0), stop=(c == M_PASSES - 1), **operands
+                        out=y_ps[:, t, :], start=(c == 0), stop=(c == M_PASSES - 1), **operands(t, c)
                     )
+            for t in range(PACK):
+                for c in range(M_PASSES):
                     nc.tensor.matmul_mx(
                         out=col_sum_ps_of[b][:],
                         start=(g == 0 and t == 0 and c == 0),
                         stop=(g == N_PASSES - 1 and t == PACK - 1 and c == M_PASSES - 1),
-                        **operands,
+                        **operands(t, c),
                     )
 
         def round_y(step):

@@ -24,7 +24,7 @@ N_PASSES = N_COLS // K_PASS
 
 VECTOR_COLS = 272
 RUN = 4
-LOAD_PARTS = 2
+LOAD_PARTS = 1
 
 FLOPS = 2 * BATCH * N_COLS * M_ROWS * PROJ + 2 * BATCH * PROJ * N_COLS * PROJ
 

@@ -22,9 +22,12 @@ K_PASS = P * PACK
 M_PASSES = M_ROWS // K_PASS
 N_PASSES = N_COLS // K_PASS
 
-VECTOR_COLS = 272
+VECTOR_COLS = 256
+VECTOR_COLS_BESIDE_Y = 336
+ROUND_LAG = 2
 RUN = 4
-LOAD_PARTS = 1
+LOAD_PARTS = 2
+FIRST_LOAD_PARTS = 4
 
 FLOPS = 2 * BATCH * N_COLS * M_ROWS * PROJ + 2 * BATCH * PROJ * N_COLS * PROJ
 
@@ -55,15 +58,21 @@ def tile_selfprojection_pb_t_kernel(
 
         x_rows = {}
 
-        def load_x(b, c):
-            x_rows[b, c] = keep.tile([P, PACK, N_COLS], BF16, name="x_rows_%d_%d" % (b, c))
+        def load_x(b, c, parts):
             source = x[b, c * K_PASS : (c + 1) * K_PASS, :].rearrange("(p j) n -> p j n", j=PACK)
-            width = N_COLS // LOAD_PARTS
-            for part in range(LOAD_PARTS):
-                cols = slice(part * width, (part + 1) * width)
-                nc.sync.dma_start(out=x_rows[b, c][:, :, cols], in_=source[:, :, cols])
+            groups = N_PASSES // parts
+            for part in range(parts):
+                rows = keep.tile(
+                    [P, PACK, groups * K_PASS], BF16, name="x_rows_%d_%d_%d" % (b, c, part)
+                )
+                first = part * groups
+                nc.sync.dma_start(
+                    out=rows[:], in_=source[:, :, first * K_PASS : (first + groups) * K_PASS]
+                )
+                for g in range(groups):
+                    x_rows[b, c, first + g] = rows[:, :, g * K_PASS : (g + 1) * K_PASS]
 
-        load_x(0, 0)
+        load_x(0, 0, FIRST_LOAD_PARTS)
         xj_rows = keep.tile([P, M_PASSES, PACK, PROJ], BF16)
         nc.sync.dma_start(
             out=xj_rows[:], in_=permuted_xj_y.rearrange("(c p j) w -> p c j w", p=P, j=PACK)
@@ -81,10 +90,10 @@ def tile_selfprojection_pb_t_kernel(
         nc.sync.dma_start(out=gamma_c[:], in_=gamma_p_sum.partition_broadcast(BATCH))
         beta_c = keep.tile([BATCH, PROJ], BF16)
         nc.sync.dma_start(out=beta_c[:], in_=beta_p_sum.partition_broadcast(BATCH))
-        load_x(0, 1)
+        load_x(0, 1, LOAD_PARTS)
         for b in range(1, BATCH):
             for c in range(M_PASSES):
-                load_x(b, c)
+                load_x(b, c, LOAD_PARTS)
 
         xj_grouped = keep.tile([P, M_PASSES, PROJ, PACK], BF16, align_bytes=64)
         xj_codes = keep.tile([P, M_PASSES, PROJ], U32, align_bytes=64)
@@ -150,13 +159,12 @@ def tile_selfprojection_pb_t_kernel(
             piece = piece_at(step)
             if piece is None:
                 return
-            b, c, g = piece
             x_grouped = stage.tile([P, K_PASS, PACK], BF16, align_bytes=64)
             x_grouped_of[piece] = x_grouped
-            rows = x_rows[b, c][:, :, g * K_PASS : (g + 1) * K_PASS]
-            source = rows.rearrange("p j (q i) -> p q j i", i=RUN)
+            source = x_rows[piece].rearrange("p j (q i) -> p q j i", i=RUN)
             target = x_grouped[:].rearrange("p (q i) j -> p q j i", i=RUN)
-            split = VECTOR_COLS // RUN
+            beside_y = group_at(step - ROUND_LAG) is not None
+            split = (VECTOR_COLS_BESIDE_Y if beside_y else VECTOR_COLS) // RUN
             nc.vector.tensor_copy(out=target[:, :split], in_=source[:, :split])
             nc.scalar.copy(out=target[:, split:], in_=source[:, split:])
 
@@ -337,8 +345,8 @@ def tile_selfprojection_pb_t_kernel(
             regroup_x(step)
             quantise_x(step - 1)
             project_x(step - 1)
-            round_y(step - 2)
-            add_col_sum(step - 2)
+            round_y(step - ROUND_LAG)
+            add_col_sum(step - ROUND_LAG)
             contract_y(step - 3)
             normalise_c(step - 3, 0)
             normalise_z(step - 4, 0)

@@ -22,12 +22,13 @@ K_PASS = P * PACK
 M_PASSES = M_ROWS // K_PASS
 N_PASSES = N_COLS // K_PASS
 
-VECTOR_COLS = 256
-VECTOR_COLS_BESIDE_Y = 336
+PIECE_COLS = 1024
+FIRST_PIECES = (256, 256, 512)
+LAST_PIECES = (512, 512)
+VECTOR_SHARE = 60
+VECTOR_SHARE_BESIDE_Y = 84
 ROUND_LAG = 2
 RUN = 4
-LOAD_PARTS = 2
-FIRST_LOAD_PARTS = 4
 
 FLOPS = 2 * BATCH * N_COLS * M_ROWS * PROJ + 2 * BATCH * PROJ * N_COLS * PROJ
 
@@ -56,23 +57,29 @@ def tile_selfprojection_pb_t_kernel(
         for b in range(BATCH):
             nc.vector.memset(select[:, b, b : b + 1], 1.0)
 
+        pieces = []
+        for b in range(BATCH):
+            for first in range(0, N_COLS, PIECE_COLS):
+                for c in range(M_PASSES):
+                    widths = (PIECE_COLS,)
+                    if not pieces:
+                        widths = FIRST_PIECES
+                    if (b, first, c) == (BATCH - 1, N_COLS - PIECE_COLS, M_PASSES - 1):
+                        widths = LAST_PIECES
+                    for i, width in enumerate(widths):
+                        pieces.append((b, c, first + sum(widths[:i]), width))
+
         x_rows = {}
 
-        def load_x(b, c, parts):
+        def load_x(piece):
+            b, c, first, width = piece
             source = x[b, c * K_PASS : (c + 1) * K_PASS, :].rearrange("(p j) n -> p j n", j=PACK)
-            groups = N_PASSES // parts
-            for part in range(parts):
-                rows = keep.tile(
-                    [P, PACK, groups * K_PASS], BF16, name="x_rows_%d_%d_%d" % (b, c, part)
-                )
-                first = part * groups
-                nc.sync.dma_start(
-                    out=rows[:], in_=source[:, :, first * K_PASS : (first + groups) * K_PASS]
-                )
-                for g in range(groups):
-                    x_rows[b, c, first + g] = rows[:, :, g * K_PASS : (g + 1) * K_PASS]
+            rows = keep.tile([P, PACK, width], BF16, name="x_rows_%d_%d_%d" % (b, c, first))
+            nc.sync.dma_start(out=rows[:], in_=source[:, :, first : first + width])
+            x_rows[piece] = rows
 
-        load_x(0, 0, FIRST_LOAD_PARTS)
+        for piece in pieces[: len(FIRST_PIECES)]:
+            load_x(piece)
         xj_rows = keep.tile([P, M_PASSES, PACK, PROJ], BF16)
         nc.sync.dma_start(
             out=xj_rows[:], in_=permuted_xj_y.rearrange("(c p j) w -> p c j w", p=P, j=PACK)
@@ -90,10 +97,8 @@ def tile_selfprojection_pb_t_kernel(
         nc.sync.dma_start(out=gamma_c[:], in_=gamma_p_sum.partition_broadcast(BATCH))
         beta_c = keep.tile([BATCH, PROJ], BF16)
         nc.sync.dma_start(out=beta_c[:], in_=beta_p_sum.partition_broadcast(BATCH))
-        load_x(0, 1, LOAD_PARTS)
-        for b in range(1, BATCH):
-            for c in range(M_PASSES):
-                load_x(b, c, LOAD_PARTS)
+        for piece in pieces[len(FIRST_PIECES) :]:
+            load_x(piece)
 
         xj_grouped = keep.tile([P, M_PASSES, PROJ, PACK], BF16, align_bytes=64)
         xj_codes = keep.tile([P, M_PASSES, PROJ], U32, align_bytes=64)
@@ -125,24 +130,22 @@ def tile_selfprojection_pb_t_kernel(
                 in_=xi_grouped[:].rearrange("p g w t -> p (g w t)"),
             )
 
-        pieces = [
-            (b, c, g) for b in range(BATCH) for c in range(M_PASSES) for g in range(N_PASSES)
-        ]
+        last_step_of = {}
+        for step, (b, c, first, width) in enumerate(pieces):
+            for g in range(first // K_PASS, (first + width - 1) // K_PASS + 1):
+                last_step_of[b, g] = step
 
         def piece_at(step):
             return pieces[step] if 0 <= step < len(pieces) else None
 
-        def group_at(step):
-            piece = piece_at(step)
-            if piece is None or piece[1] != M_PASSES - 1:
-                return None
-            return piece[0], piece[2]
+        def groups_at(step):
+            return [group for group in sorted(last_step_of) if last_step_of[group] == step]
 
         def batch_at(step):
-            group = group_at(step)
-            if group is None or group[1] != N_PASSES - 1:
-                return None
-            return group[0]
+            for b, g in groups_at(step):
+                if g == N_PASSES - 1:
+                    return b
+            return None
 
         x_grouped_of = {}
         x_codes_of = {}
@@ -159,12 +162,13 @@ def tile_selfprojection_pb_t_kernel(
             piece = piece_at(step)
             if piece is None:
                 return
-            x_grouped = stage.tile([P, K_PASS, PACK], BF16, align_bytes=64)
+            width = piece[3]
+            x_grouped = stage.tile([P, width, PACK], BF16, align_bytes=64)
             x_grouped_of[piece] = x_grouped
-            source = x_rows[piece].rearrange("p j (q i) -> p q j i", i=RUN)
+            source = x_rows[piece][:].rearrange("p j (q i) -> p q j i", i=RUN)
             target = x_grouped[:].rearrange("p (q i) j -> p q j i", i=RUN)
-            beside_y = group_at(step - ROUND_LAG) is not None
-            split = (VECTOR_COLS_BESIDE_Y if beside_y else VECTOR_COLS) // RUN
+            share = VECTOR_SHARE_BESIDE_Y if groups_at(step - ROUND_LAG) else VECTOR_SHARE
+            split = width * share // P // RUN
             nc.vector.tensor_copy(out=target[:, :split], in_=source[:, :split])
             nc.scalar.copy(out=target[:, split:], in_=source[:, split:])
 
@@ -172,15 +176,15 @@ def tile_selfprojection_pb_t_kernel(
             piece = piece_at(step)
             if piece is None:
                 return
-            b, c, g = piece
-            if c == 0 and g == 0:
+            b, c, first, width = piece
+            if c == 0 and first == 0:
                 x_codes_of[b] = codes_pool.tile(
                     [P, M_PASSES, N_COLS], U32, align_bytes=64, name="x_codes", tag="x_codes"
                 )
                 x_scales_of[b] = codes_pool.tile(
                     [P, M_PASSES, N_COLS], U8, align_bytes=64, name="x_scales", tag="x_scales"
                 )
-            cols = slice(g * K_PASS, (g + 1) * K_PASS)
+            cols = slice(first, first + width)
             nc.vector.quantize_mx(
                 out=x_codes_of[b][:, c, cols].bitcast(FP8X4),
                 scales=x_scales_of[b][:, c, cols],
@@ -188,16 +192,7 @@ def tile_selfprojection_pb_t_kernel(
             )
 
         def project_x(step):
-            group = group_at(step)
-            if group is None:
-                return
-            b, g = group
-            y_ps = psum_y.tile([P, PACK, PROJ], F32)
-            y_ps_of[group] = y_ps
-            if g == 0:
-                col_sum_ps_of[b] = psum_one.tile([P, PROJ], F32, name="col_sum_ps", tag="col_sum_ps")
-
-            def operands(t, c):
+            def operands(b, g, t, c):
                 cols = slice(g * K_PASS + t * P, g * K_PASS + (t + 1) * P)
                 return dict(
                     lhsT=x_codes_of[b][:, c, cols].bitcast(FP8X4),
@@ -206,27 +201,39 @@ def tile_selfprojection_pb_t_kernel(
                     rhs_scale=xj_scales[:, c, :],
                 )
 
-            for t in range(PACK):
-                for c in range(M_PASSES):
-                    nc.tensor.matmul_mx(
-                        out=y_ps[:, t, :], start=(c == 0), stop=(c == M_PASSES - 1), **operands(t, c)
+            for b, g in groups_at(step):
+                y_ps = psum_y.tile([P, PACK, PROJ], F32)
+                y_ps_of[b, g] = y_ps
+                for t in range(PACK):
+                    for c in range(M_PASSES):
+                        nc.tensor.matmul_mx(
+                            out=y_ps[:, t, :], start=(c == 0), stop=(c == M_PASSES - 1),
+                            **operands(b, g, t, c),
+                        )
+            for b, g in groups_at(step):
+                if g == 0:
+                    col_sum_ps_of[b] = psum_one.tile(
+                        [P, PROJ], F32, name="col_sum_ps", tag="col_sum_ps"
                     )
-            for t in range(PACK):
-                for c in range(M_PASSES):
-                    nc.tensor.matmul_mx(
-                        out=col_sum_ps_of[b][:],
-                        start=(g == 0 and t == 0 and c == 0),
-                        stop=(g == N_PASSES - 1 and t == PACK - 1 and c == M_PASSES - 1),
-                        **operands(t, c),
-                    )
+                for t in range(PACK):
+                    for c in range(M_PASSES):
+                        nc.tensor.matmul_mx(
+                            out=col_sum_ps_of[b][:],
+                            start=(g == 0 and t == 0 and c == 0),
+                            stop=(g == N_PASSES - 1 and t == PACK - 1 and c == M_PASSES - 1),
+                            **operands(b, g, t, c),
+                        )
 
         def round_y(step):
-            group = group_at(step)
-            if group is None:
+            groups = groups_at(step)
+            if not groups:
                 return
-            y_grouped = stage.tile([P, PROJ, PACK], BF16, align_bytes=64)
-            y_grouped_of[group] = y_grouped
-            nc.scalar.copy(out=y_grouped[:], in_=y_ps_of[group][:].rearrange("p t w -> p w t"))
+            y_grouped = stage.tile([P, len(groups), PROJ, PACK], BF16, align_bytes=64)
+            y_grouped_of[step] = y_grouped
+            for i, group in enumerate(groups):
+                nc.scalar.copy(
+                    out=y_grouped[:, i], in_=y_ps_of[group][:].rearrange("p t w -> p w t")
+                )
 
         def add_col_sum(step):
             b = batch_at(step)
@@ -240,33 +247,34 @@ def tile_selfprojection_pb_t_kernel(
             )
 
         def contract_y(step):
-            group = group_at(step)
-            if group is None:
+            groups = groups_at(step)
+            if not groups:
                 return
-            b, g = group
-            y_codes = stage.tile([P, PROJ], U32, align_bytes=64)
-            y_scales = stage.tile([P, PROJ], U8, align_bytes=64)
+            y_codes = stage.tile([P, len(groups), PROJ], U32, align_bytes=64)
+            y_scales = stage.tile([P, len(groups), PROJ], U8, align_bytes=64)
             nc.vector.quantize_mx(
-                out=y_codes[:].bitcast(FP8X4),
-                scales=y_scales[:],
-                in_=y_grouped_of[group][:].rearrange("p w t -> p (w t)"),
+                out=y_codes[:].rearrange("p i w -> p (i w)").bitcast(FP8X4),
+                scales=y_scales[:].rearrange("p i w -> p (i w)"),
+                in_=y_grouped_of[step][:].rearrange("p i w t -> p (i w t)"),
             )
-            if g == 0:
-                z_ps_of[b] = psum_one.tile([P, PROJ], F32, name="z_ps", tag="z_ps")
-            nc.tensor.matmul_mx(
-                out=z_ps_of[b][:],
-                lhsT=xi_codes[:, g, :].bitcast(FP8X4),
-                lhsT_scale=xi_scales[:, g, :],
-                rhs=y_codes[:].bitcast(FP8X4),
-                rhs_scale=y_scales[:],
-                start=(g == 0),
-                stop=(g == N_PASSES - 1),
-            )
+            for i, (b, g) in enumerate(groups):
+                if g == 0:
+                    z_ps_of[b] = psum_one.tile([P, PROJ], F32, name="z_ps", tag="z_ps")
+                nc.tensor.matmul_mx(
+                    out=z_ps_of[b][:],
+                    lhsT=xi_codes[:, g, :].bitcast(FP8X4),
+                    lhsT_scale=xi_scales[:, g, :],
+                    rhs=y_codes[:, i, :].bitcast(FP8X4),
+                    rhs_scale=y_scales[:, i, :],
+                    start=(g == 0),
+                    stop=(g == N_PASSES - 1),
+                )
 
 
         def small_tile(what, name, rows, cols):
             label = what + "_" + name
-            return finish.tile([rows, cols], F32, name=label, tag=label)
+            pool = keep if what == "c" else finish
+            return pool.tile([rows, cols], F32, name=label, tag=label)
 
         def sum_values(what, rows, values_ps, add_up, tiles):
             tiles["values"] = small_tile(what, "values", rows, PROJ)
@@ -340,7 +348,7 @@ def tile_selfprojection_pb_t_kernel(
 
         STAGES = 7
         for step in range(len(pieces) + STAGES - 1):
-            if step == N_PASSES:
+            if step == len(FIRST_PIECES):
                 prepare_small_operands()
             regroup_x(step)
             quantise_x(step - 1)

@@ -25,8 +25,8 @@ N_PASSES = N_COLS // K_PASS
 PIECE_COLS = 1024
 FIRST_PIECES = (256, 256, 512)
 LAST_PIECES = (512, 512)
-VECTOR_SHARE = 60
-VECTOR_SHARE_BESIDE_Y = 84
+VECTOR_SHARE = 68
+VECTOR_SHARE_BESIDE_Y = 92
 ROUND_LAG = 2
 RUN = 4
 

@@ -154,8 +154,6 @@ def tile_selfprojection_pb_t_kernel(
         y_grouped_of = {}
         col_sum_ps_of = {}
         z_ps_of = {}
-        z_tiles_of = {}
-        c_tiles = {}
         c_ps = psum_one.tile([P, PROJ], F32)
 
         def regroup_x(step):
@@ -192,8 +190,12 @@ def tile_selfprojection_pb_t_kernel(
             )
 
         def project_x(step):
-            def operands(b, g, t, c):
-                cols = slice(g * K_PASS + t * P, g * K_PASS + (t + 1) * P)
+            piece = piece_at(step)
+            if piece is None:
+                return
+
+            def operands(b, c, first):
+                cols = slice(first, first + P)
                 return dict(
                     lhsT=x_codes_of[b][:, c, cols].bitcast(FP8X4),
                     lhsT_scale=x_scales_of[b][:, c, cols],
@@ -208,21 +210,22 @@ def tile_selfprojection_pb_t_kernel(
                     for c in range(M_PASSES):
                         nc.tensor.matmul_mx(
                             out=y_ps[:, t, :], start=(c == 0), stop=(c == M_PASSES - 1),
-                            **operands(b, g, t, c),
+                            **operands(b, c, g * K_PASS + t * P),
                         )
-            for b, g in groups_at(step):
-                if g == 0:
+            if step < len(FIRST_PIECES) - 1:
+                return
+            for b, c, first, width in pieces[0 if step < len(FIRST_PIECES) else step : step + 1]:
+                if c == 0 and first == 0:
                     col_sum_ps_of[b] = psum_one.tile(
                         [P, PROJ], F32, name="col_sum_ps", tag="col_sum_ps"
                     )
-                for t in range(PACK):
-                    for c in range(M_PASSES):
-                        nc.tensor.matmul_mx(
-                            out=col_sum_ps_of[b][:],
-                            start=(g == 0 and t == 0 and c == 0),
-                            stop=(g == N_PASSES - 1 and t == PACK - 1 and c == M_PASSES - 1),
-                            **operands(b, g, t, c),
-                        )
+                for tile_first in range(first, first + width, P):
+                    nc.tensor.matmul_mx(
+                        out=col_sum_ps_of[b][:],
+                        start=(c == 0 and tile_first == 0),
+                        stop=(batch_at(step) == b and tile_first == first + width - P),
+                        **operands(b, c, tile_first),
+                    )
 
         def round_y(step):
             groups = groups_at(step)
@@ -240,7 +243,7 @@ def tile_selfprojection_pb_t_kernel(
             if b is None:
                 return
             col_sum = finish.tile([P, PROJ], F32)
-            nc.vector.tensor_copy(out=col_sum[:], in_=col_sum_ps_of[b][:])
+            nc.scalar.copy(out=col_sum[:], in_=col_sum_ps_of[b][:])
             nc.tensor.matmul(
                 out=c_ps[:], lhsT=select[:, b, :], rhs=col_sum[:],
                 start=(b == 0), stop=(b == BATCH - 1),
@@ -271,51 +274,6 @@ def tile_selfprojection_pb_t_kernel(
                 )
 
 
-        def small_tile(what, name, rows, cols):
-            label = what + "_" + name
-            pool = keep if what == "c" else finish
-            return pool.tile([rows, cols], F32, name=label, tag=label)
-
-        def sum_values(what, rows, values_ps, add_up, tiles):
-            tiles["values"] = small_tile(what, "values", rows, PROJ)
-            row_sum = small_tile(what, "row_sum", rows, 1)
-            nc.scalar.activation(
-                out=tiles["values"][:], in_=values_ps, func=ACT.Copy, accum_out=row_sum[:]
-            )
-            tiles["total"] = add_up("total", row_sum)
-
-        def centre_values(what, rows, count, gamma, add_up, tiles):
-            neg_mean = small_tile(what, "neg_mean", rows, 1)
-            nc.vector.tensor_scalar_mul(out=neg_mean[:], in0=tiles["total"][:], scalar1=-1.0 / count)
-            squares = small_tile(what, "squares", rows, PROJ)
-            row_squares = small_tile(what, "row_squares", rows, 1)
-            nc.scalar.activation(
-                out=squares[:], in_=tiles["values"][:], func=ACT.Square, bias=neg_mean[:],
-                accum_out=row_squares[:],
-            )
-            tiles["total_squares"] = add_up("total_squares", row_squares)
-            tiles["gained"] = small_tile(what, "gained", rows, PROJ)
-            nc.vector.scalar_tensor_tensor(
-                out=tiles["gained"][:], in0=tiles["values"][:], scalar=neg_mean[:], in1=gamma,
-                op0=ALU.add, op1=ALU.mult,
-            )
-
-        def scale_values(what, rows, count, beta, tiles, destination):
-            std = small_tile(what, "std", rows, 1)
-            nc.scalar.activation(
-                out=std[:], in_=tiles["total_squares"][:], func=ACT.Sqrt, scale=1.0 / (count - 1)
-            )
-            std_eps = small_tile(what, "std_eps", rows, 1)
-            nc.vector.tensor_scalar_add(out=std_eps[:], in0=std[:], scalar1=EPS)
-            inverse = small_tile(what, "inverse", rows, 1)
-            nc.vector.reciprocal(out=inverse[:], in_=std_eps[:])
-            result = small_tile(what, "result", rows, PROJ)
-            nc.vector.scalar_tensor_tensor(
-                out=result[:], in0=tiles["gained"][:], scalar=inverse[:], in1=beta,
-                op0=ALU.mult, op1=ALU.add,
-            )
-            nc.sync.dma_start(out=destination, in_=result[:])
-
         def over_partitions(name, column):
             total_ps = psum_one.tile([P, 1], F32, name=name, tag=name)
             nc.tensor.matmul(out=total_ps[:], lhsT=ones[:], rhs=column[:], start=True, stop=True)
@@ -324,30 +282,87 @@ def tile_selfprojection_pb_t_kernel(
         def within_partition(name, column):
             return column
 
-        def normalise_z(step, part):
+        z_std = keep.tile([P, BATCH], F32)
+        z_std_eps = keep.tile([P, BATCH], F32)
+        z_inverse = keep.tile([P, BATCH], F32)
+        c_std = keep.tile([BATCH, 1], F32)
+        c_std_eps = keep.tile([BATCH, 1], F32)
+        c_inverse = keep.tile([BATCH, 1], F32)
+        norm_of = {
+            b: dict(
+                what="z", rows=P, count=PROJ * PROJ, gamma=gamma_z[:], beta=beta_z[:],
+                destination=out_0[b], add_up=over_partitions,
+                std=z_std[:, b : b + 1], inverse=z_inverse[:, b : b + 1],
+            )
+            for b in range(BATCH)
+        }
+        norm_c = dict(
+            what="c", rows=BATCH, count=PROJ, gamma=gamma_c[:], beta=beta_c_plus_1[:],
+            destination=out_1, add_up=within_partition, std=c_std[:], inverse=c_inverse[:],
+        )
+
+        def small_tile(norm, name, cols):
+            label = norm["what"] + "_" + name
+            pool = keep if norm["what"] == "c" else finish
+            return pool.tile([norm["rows"], cols], F32, name=label, tag=label)
+
+        def sum_values(norm, values_ps):
+            norm["values"] = small_tile(norm, "values", PROJ)
+            row_sum = small_tile(norm, "row_sum", 1)
+            nc.scalar.activation(
+                out=norm["values"][:], in_=values_ps, func=ACT.Copy, accum_out=row_sum[:]
+            )
+            norm["total"] = norm["add_up"]("total", row_sum)
+
+        def negate_mean(norm):
+            norm["neg_mean"] = small_tile(norm, "neg_mean", 1)
+            nc.scalar.activation(
+                out=norm["neg_mean"][:], in_=norm["total"][:], func=ACT.Copy,
+                scale=-1.0 / norm["count"],
+            )
+
+        def sum_squares(norm):
+            squares = small_tile(norm, "squares", PROJ)
+            row_squares = small_tile(norm, "row_squares", 1)
+            nc.scalar.activation(
+                out=squares[:], in_=norm["values"][:], func=ACT.Square, bias=norm["neg_mean"][:],
+                accum_out=row_squares[:],
+            )
+            norm["total_squares"] = norm["add_up"]("total_squares", row_squares)
+
+        def take_root(norm):
+            nc.scalar.activation(
+                out=norm["std"], in_=norm["total_squares"][:], func=ACT.Sqrt,
+                scale=1.0 / (norm["count"] - 1),
+            )
+
+        def gain(norm):
+            norm["gained"] = small_tile(norm, "gained", PROJ)
+            nc.vector.scalar_tensor_tensor(
+                out=norm["gained"][:], in0=norm["values"][:], scalar=norm["neg_mean"][:],
+                in1=norm["gamma"], op0=ALU.add, op1=ALU.mult,
+            )
+
+        def invert(std, std_eps, inverse):
+            nc.vector.tensor_scalar_add(out=std_eps, in0=std, scalar1=EPS)
+            nc.vector.reciprocal(out=inverse, in_=std_eps)
+
+        def finish_values(norm):
+            result = small_tile(norm, "result", PROJ)
+            nc.vector.scalar_tensor_tensor(
+                out=result[:], in0=norm["gained"][:], scalar=norm["inverse"], in1=norm["beta"],
+                op0=ALU.mult, op1=ALU.add,
+            )
+            nc.sync.dma_start(out=norm["destination"], in_=result[:])
+
+        def for_batch_at(step, part):
             b = batch_at(step)
-            if b is None:
-                return
-            if part == 0:
-                z_tiles_of[b] = {}
-                sum_values("z", P, z_ps_of[b][:], over_partitions, z_tiles_of[b])
-            if part == 1:
-                centre_values("z", P, PROJ * PROJ, gamma_z[:], over_partitions, z_tiles_of[b])
-            if part == 2:
-                scale_values("z", P, PROJ * PROJ, beta_z[:], z_tiles_of[b], out_0[b])
+            if b is not None:
+                part(b)
 
-        def normalise_c(step, part):
-            if step != len(pieces) - 1:
-                return
-            if part == 0:
-                sum_values("c", BATCH, c_ps[:BATCH, :], within_partition, c_tiles)
-            if part == 1:
-                centre_values("c", BATCH, PROJ, gamma_c[:], within_partition, c_tiles)
-            if part == 2:
-                scale_values("c", BATCH, PROJ, beta_c_plus_1[:], c_tiles, out_1)
-
-        STAGES = 7
-        for step in range(len(pieces) + STAGES - 1):
+        last = len(pieces) - 1
+        final = BATCH - 1
+        for step in range(last + 1):
             if step == len(FIRST_PIECES):
                 prepare_small_operands()
             regroup_x(step)
@@ -356,9 +371,36 @@ def tile_selfprojection_pb_t_kernel(
             round_y(step - ROUND_LAG)
             add_col_sum(step - ROUND_LAG)
             contract_y(step - 3)
-            normalise_c(step - 3, 0)
-            normalise_z(step - 4, 0)
-            normalise_c(step - 4, 1)
-            normalise_z(step - 5, 1)
-            normalise_c(step - 5, 2)
-            normalise_z(step - 6, 2)
+            for_batch_at(step - 4, lambda b: sum_values(norm_of[b], z_ps_of[b][:]))
+            for_batch_at(step - 5, lambda b: negate_mean(norm_of[b]))
+            for_batch_at(step - 5, lambda b: sum_squares(norm_of[b]))
+            for_batch_at(step - 6, lambda b: take_root(norm_of[b]))
+
+        quantise_x(last)
+        project_x(last)
+        take_root(norm_of[final - 1])
+        gain(norm_of[0])
+        round_y(last - 1)
+        contract_y(last - 1)
+        gain(norm_of[1])
+        round_y(last)
+        contract_y(last)
+        add_col_sum(last)
+        sum_values(norm_of[final], z_ps_of[final][:])
+        gain(norm_of[2])
+        invert(z_std[:, :final], z_std_eps[:, :final], z_inverse[:, :final])
+        for b in range(final):
+            finish_values(norm_of[b])
+        sum_values(norm_c, c_ps[:BATCH, :])
+        negate_mean(norm_c)
+        negate_mean(norm_of[final])
+        sum_squares(norm_of[final])
+        sum_squares(norm_c)
+        gain(norm_of[final])
+        gain(norm_c)
+        take_root(norm_of[final])
+        take_root(norm_c)
+        invert(z_std[:, final:], z_std_eps[:, final:], z_inverse[:, final:])
+        finish_values(norm_of[final])
+        invert(c_std[:], c_std_eps[:], c_inverse[:])
+        finish_values(norm_c)

@@ -25,8 +25,8 @@ N_PASSES = N_COLS // K_PASS
 PIECE_COLS = 1024
 FIRST_PIECES = (256, 256, 512)
 LAST_PIECES = (512, 512)
-VECTOR_SHARE = 68
-VECTOR_SHARE_BESIDE_Y = 92
+VECTOR_SHARE = 60
+VECTOR_SHARE_BESIDE_Y = 84
 ROUND_LAG = 2
 RUN = 4
 
@@ -274,91 +274,87 @@ def tile_selfprojection_pb_t_kernel(
                 )
 
 
-        def over_partitions(name, column):
-            total_ps = psum_one.tile([P, 1], F32, name=name, tag=name)
-            nc.tensor.matmul(out=total_ps[:], lhsT=ones[:], rhs=column[:], start=True, stop=True)
-            return total_ps
-
-        def within_partition(name, column):
-            return column
-
-        z_std = keep.tile([P, BATCH], F32)
-        z_std_eps = keep.tile([P, BATCH], F32)
-        z_inverse = keep.tile([P, BATCH], F32)
-        c_std = keep.tile([BATCH, 1], F32)
-        c_std_eps = keep.tile([BATCH, 1], F32)
-        c_inverse = keep.tile([BATCH, 1], F32)
-        norm_of = {
-            b: dict(
-                what="z", rows=P, count=PROJ * PROJ, gamma=gamma_z[:], beta=beta_z[:],
-                destination=out_0[b], add_up=over_partitions,
-                std=z_std[:, b : b + 1], inverse=z_inverse[:, b : b + 1],
+        def statistics(what, rows, columns, count, gamma, beta, destinations):
+            norm = dict(
+                what=what, rows=rows, count=count, gamma=gamma, beta=beta,
+                destinations=destinations, values={}, gained={},
             )
-            for b in range(BATCH)
-        }
-        norm_c = dict(
-            what="c", rows=BATCH, count=PROJ, gamma=gamma_c[:], beta=beta_c_plus_1[:],
-            destination=out_1, add_up=within_partition, std=c_std[:], inverse=c_inverse[:],
-        )
+            for name in ("row_sum", "neg_mean", "row_squares", "std", "std_eps", "inverse"):
+                label = what + "_" + name
+                norm[name] = keep.tile([rows, columns], F32, name=label, tag=label)
+            return norm
 
-        def small_tile(norm, name, cols):
+        z_norm = statistics(
+            "z", P, BATCH, PROJ * PROJ, gamma_z[:], beta_z[:], [out_0[b] for b in range(BATCH)]
+        )
+        c_norm = statistics("c", BATCH, 1, PROJ, gamma_c[:], beta_c_plus_1[:], [out_1])
+        for name in ("row_sum", "row_squares"):
+            label = "z_total_" + name
+            z_norm["total_" + name] = psum_one.tile([P, BATCH], F32, name=label, tag=label)
+            c_norm["total_" + name] = c_norm[name]
+
+        def add_up(norm, name, low, high):
+            if norm["what"] == "z":
+                nc.tensor.matmul(
+                    out=norm["total_" + name][:, low:high], lhsT=ones[:],
+                    rhs=norm[name][:, low:high], start=True, stop=True,
+                )
+
+        def wide_tile(norm, name):
             label = norm["what"] + "_" + name
             pool = keep if norm["what"] == "c" else finish
-            return pool.tile([norm["rows"], cols], F32, name=label, tag=label)
+            return pool.tile([norm["rows"], PROJ], F32, name=label, tag=label)
 
-        def sum_values(norm, values_ps):
-            norm["values"] = small_tile(norm, "values", PROJ)
-            row_sum = small_tile(norm, "row_sum", 1)
+        def sum_values(norm, k, values_ps):
+            norm["values"][k] = wide_tile(norm, "values")
             nc.scalar.activation(
-                out=norm["values"][:], in_=values_ps, func=ACT.Copy, accum_out=row_sum[:]
+                out=norm["values"][k][:], in_=values_ps, func=ACT.Copy,
+                accum_out=norm["row_sum"][:, k : k + 1],
             )
-            norm["total"] = norm["add_up"]("total", row_sum)
+            add_up(norm, "row_sum", k, k + 1)
 
-        def negate_mean(norm):
-            norm["neg_mean"] = small_tile(norm, "neg_mean", 1)
+        def negate_means(norm, low, high):
             nc.scalar.activation(
-                out=norm["neg_mean"][:], in_=norm["total"][:], func=ACT.Copy,
-                scale=-1.0 / norm["count"],
-            )
-
-        def sum_squares(norm):
-            squares = small_tile(norm, "squares", PROJ)
-            row_squares = small_tile(norm, "row_squares", 1)
-            nc.scalar.activation(
-                out=squares[:], in_=norm["values"][:], func=ACT.Square, bias=norm["neg_mean"][:],
-                accum_out=row_squares[:],
-            )
-            norm["total_squares"] = norm["add_up"]("total_squares", row_squares)
-
-        def take_root(norm):
-            nc.scalar.activation(
-                out=norm["std"], in_=norm["total_squares"][:], func=ACT.Sqrt,
-                scale=1.0 / (norm["count"] - 1),
+                out=norm["neg_mean"][:, low:high], in_=norm["total_row_sum"][:, low:high],
+                func=ACT.Copy, scale=-1.0 / norm["count"],
             )
 
-        def gain(norm):
-            norm["gained"] = small_tile(norm, "gained", PROJ)
+        def sum_squares(norm, k):
+            squares = wide_tile(norm, "squares")
+            nc.scalar.activation(
+                out=squares[:], in_=norm["values"][k][:], func=ACT.Square,
+                bias=norm["neg_mean"][:, k : k + 1], accum_out=norm["row_squares"][:, k : k + 1],
+            )
+
+        def take_roots(norm, low, high):
+            nc.scalar.activation(
+                out=norm["std"][:, low:high], in_=norm["total_row_squares"][:, low:high],
+                func=ACT.Sqrt, scale=1.0 / (norm["count"] - 1),
+            )
+
+        def gain(norm, k):
+            norm["gained"][k] = wide_tile(norm, "gained")
             nc.vector.scalar_tensor_tensor(
-                out=norm["gained"][:], in0=norm["values"][:], scalar=norm["neg_mean"][:],
-                in1=norm["gamma"], op0=ALU.add, op1=ALU.mult,
+                out=norm["gained"][k][:], in0=norm["values"][k][:],
+                scalar=norm["neg_mean"][:, k : k + 1], in1=norm["gamma"],
+                op0=ALU.add, op1=ALU.mult,
             )
 
-        def invert(std, std_eps, inverse):
-            nc.vector.tensor_scalar_add(out=std_eps, in0=std, scalar1=EPS)
-            nc.vector.reciprocal(out=inverse, in_=std_eps)
+        def invert(norm, low, high):
+            nc.vector.tensor_scalar_add(
+                out=norm["std_eps"][:, low:high], in0=norm["std"][:, low:high], scalar1=EPS
+            )
+            nc.vector.reciprocal(
+                out=norm["inverse"][:, low:high], in_=norm["std_eps"][:, low:high]
+            )
 
-        def finish_values(norm):
-            result = small_tile(norm, "result", PROJ)
+        def finish_values(norm, k):
+            result = wide_tile(norm, "result")
             nc.vector.scalar_tensor_tensor(
-                out=result[:], in0=norm["gained"][:], scalar=norm["inverse"], in1=norm["beta"],
-                op0=ALU.mult, op1=ALU.add,
+                out=result[:], in0=norm["gained"][k][:], scalar=norm["inverse"][:, k : k + 1],
+                in1=norm["beta"], op0=ALU.mult, op1=ALU.add,
             )
-            nc.sync.dma_start(out=norm["destination"], in_=result[:])
-
-        def for_batch_at(step, part):
-            b = batch_at(step)
-            if b is not None:
-                part(b)
+            nc.sync.dma_start(out=norm["destinations"][k], in_=result[:])
 
         last = len(pieces) - 1
         final = BATCH - 1
@@ -371,36 +367,40 @@ def tile_selfprojection_pb_t_kernel(
             round_y(step - ROUND_LAG)
             add_col_sum(step - ROUND_LAG)
             contract_y(step - 3)
-            for_batch_at(step - 4, lambda b: sum_values(norm_of[b], z_ps_of[b][:]))
-            for_batch_at(step - 5, lambda b: negate_mean(norm_of[b]))
-            for_batch_at(step - 5, lambda b: sum_squares(norm_of[b]))
-            for_batch_at(step - 6, lambda b: take_root(norm_of[b]))
+            b = batch_at(step - 4)
+            if b is not None:
+                sum_values(z_norm, b, z_ps_of[b][:])
 
+        negate_means(z_norm, 0, final)
+        for b in range(final):
+            sum_squares(z_norm, b)
         quantise_x(last)
         project_x(last)
-        take_root(norm_of[final - 1])
-        gain(norm_of[0])
+        add_up(z_norm, "row_squares", 0, final)
+        gain(z_norm, 0)
         round_y(last - 1)
         contract_y(last - 1)
-        gain(norm_of[1])
+        gain(z_norm, 1)
         round_y(last)
+        take_roots(z_norm, 0, final)
         contract_y(last)
         add_col_sum(last)
-        sum_values(norm_of[final], z_ps_of[final][:])
-        gain(norm_of[2])
-        invert(z_std[:, :final], z_std_eps[:, :final], z_inverse[:, :final])
+        sum_values(z_norm, final, z_ps_of[final][:])
+        gain(z_norm, 2)
+        invert(z_norm, 0, final)
         for b in range(final):
-            finish_values(norm_of[b])
-        sum_values(norm_c, c_ps[:BATCH, :])
-        negate_mean(norm_c)
-        negate_mean(norm_of[final])
-        sum_squares(norm_of[final])
-        sum_squares(norm_c)
-        gain(norm_of[final])
-        gain(norm_c)
-        take_root(norm_of[final])
-        take_root(norm_c)
-        invert(z_std[:, final:], z_std_eps[:, final:], z_inverse[:, final:])
-        finish_values(norm_of[final])
-        invert(c_std[:], c_std_eps[:], c_inverse[:])
-        finish_values(norm_c)
+            finish_values(z_norm, b)
+        sum_values(c_norm, 0, c_ps[:BATCH, :])
+        negate_means(c_norm, 0, 1)
+        negate_means(z_norm, final, BATCH)
+        sum_squares(z_norm, final)
+        add_up(z_norm, "row_squares", final, BATCH)
+        sum_squares(c_norm, 0)
+        take_roots(c_norm, 0, 1)
+        gain(z_norm, final)
+        gain(c_norm, 0)
+        invert(c_norm, 0, 1)
+        finish_values(c_norm, 0)
+        take_roots(z_norm, final, BATCH)
+        invert(z_norm, final, BATCH)
+        finish_values(z_norm, final)

@@ -238,12 +238,12 @@ def tile_selfprojection_pb_t_kernel(
                     out=y_grouped[:, i], in_=y_ps_of[group][:].rearrange("p t w -> p w t")
                 )
 
-        def add_col_sum(step):
+        def add_col_sum(step, copy):
             b = batch_at(step)
             if b is None:
                 return
             col_sum = finish.tile([P, PROJ], F32)
-            nc.scalar.copy(out=col_sum[:], in_=col_sum_ps_of[b][:])
+            copy(out=col_sum[:], in_=col_sum_ps_of[b][:])
             nc.tensor.matmul(
                 out=c_ps[:], lhsT=select[:, b, :], rhs=col_sum[:],
                 start=(b == 0), stop=(b == BATCH - 1),
@@ -340,10 +340,12 @@ def tile_selfprojection_pb_t_kernel(
                 op0=ALU.add, op1=ALU.mult,
             )
 
-        def invert(norm, low, high):
+        def add_eps(norm, low, high):
             nc.vector.tensor_scalar_add(
                 out=norm["std_eps"][:, low:high], in0=norm["std"][:, low:high], scalar1=EPS
             )
+
+        def invert(norm, low, high):
             nc.vector.reciprocal(
                 out=norm["inverse"][:, low:high], in_=norm["std_eps"][:, low:high]
             )
@@ -365,7 +367,7 @@ def tile_selfprojection_pb_t_kernel(
             quantise_x(step - 1)
             project_x(step - 1)
             round_y(step - ROUND_LAG)
-            add_col_sum(step - ROUND_LAG)
+            add_col_sum(step - ROUND_LAG, nc.scalar.copy)
             contract_y(step - 3)
             b = batch_at(step - 4)
             if b is not None:
@@ -381,11 +383,12 @@ def tile_selfprojection_pb_t_kernel(
         round_y(last - 1)
         contract_y(last - 1)
         gain(z_norm, 1)
+        add_col_sum(last, nc.vector.tensor_copy)
         round_y(last)
         take_roots(z_norm, 0, final)
         contract_y(last)
-        add_col_sum(last)
         sum_values(z_norm, final, z_ps_of[final][:])
+        add_eps(z_norm, 0, final)
         gain(z_norm, 2)
         invert(z_norm, 0, final)
         for b in range(final):
@@ -397,10 +400,12 @@ def tile_selfprojection_pb_t_kernel(
         add_up(z_norm, "row_squares", final, BATCH)
         sum_squares(c_norm, 0)
         take_roots(c_norm, 0, 1)
+        take_roots(z_norm, final, BATCH)
         gain(z_norm, final)
         gain(c_norm, 0)
+        add_eps(c_norm, 0, 1)
+        add_eps(z_norm, final, BATCH)
         invert(c_norm, 0, 1)
-        finish_values(c_norm, 0)
-        take_roots(z_norm, final, BATCH)
         invert(z_norm, final, BATCH)
+        finish_values(c_norm, 0)
         finish_values(z_norm, final)

from contextlib import ExitStack

import concourse.mybir as mybir

F32 = mybir.dt.float32
BF16 = mybir.dt.bfloat16
U32 = mybir.dt.uint32
U8 = mybir.dt.uint8
FP8X4 = mybir.dt.float8_e4m3fn_x4
ACT = mybir.ActivationFunctionType
ALU = mybir.AluOpType

BATCH = 4
M_ROWS = 1024
N_COLS = 2048
PROJ = 128
EPS = 1e-5

P = 128
PACK = 4
K_PASS = P * PACK
M_PASSES = M_ROWS // K_PASS
N_PASSES = N_COLS // K_PASS

PIECE_COLS = 1024
FIRST_PIECES = (256, 256, 512)
LAST_PIECES = (512, 512)
VECTOR_SHARE = 60
VECTOR_SHARE_BESIDE_Y = 84
ROUND_LAG = 2
RUN = 4

FLOPS = 2 * BATCH * N_COLS * M_ROWS * PROJ + 2 * BATCH * PROJ * N_COLS * PROJ


def tile_selfprojection_pb_t_kernel(
    tc, x, permuted_xj_y, permuted_xi_y, gamma_p_sum, gamma_p, beta_p_sum, beta_p, out_0, out_1
):
    nc = tc.nc
    with ExitStack() as ctx:
        keep = ctx.enter_context(tc.tile_pool(name="keep", bufs=1))
        codes_pool = ctx.enter_context(tc.tile_pool(name="codes", bufs=2))
        stage = ctx.enter_context(tc.tile_pool(name="stage", bufs=3))
        finish = ctx.enter_context(tc.tile_pool(name="finish", bufs=BATCH))
        psum_y = ctx.enter_context(tc.psum_pool(name="psum_y", bufs=3))
        psum_one = ctx.enter_context(tc.psum_pool(name="psum_one", bufs=1))
        ctx.enter_context(tc.manual_schedule())

        warm = keep.tile([P, 1], F32)
        nc.vector.memset(warm[:], 1.0)
        nc.scalar.activation(out=warm[:], in_=warm[:], func=ACT.Sqrt)

        ones = keep.tile([P, P], F32)
        nc.vector.memset(ones[:], 1.0)
        select = keep.tile([P, BATCH, P], F32)
        nc.vector.memset(select[:], 0.0)
        for b in range(BATCH):
            nc.vector.memset(select[:, b, b : b + 1], 1.0)

        pieces = []
        for b in range(BATCH):
            for first in range(0, N_COLS, PIECE_COLS):
                for c in range(M_PASSES):
                    widths = (PIECE_COLS,)
                    if not pieces:
                        widths = FIRST_PIECES
                    if (b, first, c) == (BATCH - 1, N_COLS - PIECE_COLS, M_PASSES - 1):
                        widths = LAST_PIECES
                    for i, width in enumerate(widths):
                        pieces.append((b, c, first + sum(widths[:i]), width))

        x_rows = {}

        def load_x(piece):
            b, c, first, width = piece
            source = x[b, c * K_PASS : (c + 1) * K_PASS, :].rearrange("(p j) n -> p j n", j=PACK)
            rows = keep.tile([P, PACK, width], BF16, name="x_rows_%d_%d_%d" % (b, c, first))
            nc.sync.dma_start(out=rows[:], in_=source[:, :, first : first + width])
            x_rows[piece] = rows

        for piece in pieces[: len(FIRST_PIECES)]:
            load_x(piece)
        xj_rows = keep.tile([P, M_PASSES, PACK, PROJ], BF16)
        nc.sync.dma_start(
            out=xj_rows[:], in_=permuted_xj_y.rearrange("(c p j) w -> p c j w", p=P, j=PACK)
        )
        xi_rows = keep.tile([P, N_PASSES, PACK, PROJ], BF16)
        nc.sync.dma_start(
            out=xi_rows[:].rearrange("p g t w -> p (g t) w"),
            in_=permuted_xi_y.rearrange("(a p) w -> p a w", p=P),
        )
        gamma_z = keep.tile([P, PROJ], BF16)
        nc.sync.dma_start(out=gamma_z[:], in_=gamma_p)
        beta_z = keep.tile([P, PROJ], BF16)
        nc.sync.dma_start(out=beta_z[:], in_=beta_p)
        gamma_c = keep.tile([BATCH, PROJ], BF16)
        nc.sync.dma_start(out=gamma_c[:], in_=gamma_p_sum.partition_broadcast(BATCH))
        beta_c = keep.tile([BATCH, PROJ], BF16)
        nc.sync.dma_start(out=beta_c[:], in_=beta_p_sum.partition_broadcast(BATCH))
        for piece in pieces[len(FIRST_PIECES) :]:
            load_x(piece)

        xj_grouped = keep.tile([P, M_PASSES, PROJ, PACK], BF16, align_bytes=64)
        xj_codes = keep.tile([P, M_PASSES, PROJ], U32, align_bytes=64)
        xj_scales = keep.tile([P, M_PASSES, PROJ], U8, align_bytes=64)
        xi_grouped = keep.tile([P, N_PASSES, PROJ, PACK], BF16, align_bytes=64)
        xi_codes = keep.tile([P, N_PASSES, PROJ], U32, align_bytes=64)
        xi_scales = keep.tile([P, N_PASSES, PROJ], U8, align_bytes=64)

        beta_c_plus_1 = keep.tile([BATCH, PROJ], F32)

        def prepare_small_operands():
            half = N_PASSES // 2
            nc.vector.tensor_copy(out=xj_grouped[:], in_=xj_rows[:].rearrange("p c j w -> p c w j"))
            nc.scalar.copy(
                out=xi_grouped[:, half:], in_=xi_rows[:, half:].rearrange("p g t w -> p g w t")
            )
            nc.vector.tensor_copy(
                out=xi_grouped[:, :half], in_=xi_rows[:, :half].rearrange("p g t w -> p g w t")
            )
            nc.vector.quantize_mx(
                out=xj_codes[:].rearrange("p c w -> p (c w)").bitcast(FP8X4),
                scales=xj_scales[:].rearrange("p c w -> p (c w)"),
                in_=xj_grouped[:].rearrange("p c w j -> p (c w j)"),
            )
            nc.vector.tensor_scalar_add(out=beta_c_plus_1[:], in0=beta_c[:], scalar1=1.0)
            nc.vector.quantize_mx(
                out=xi_codes[:].rearrange("p g w -> p (g w)").bitcast(FP8X4),
                scales=xi_scales[:].rearrange("p g w -> p (g w)"),
                in_=xi_grouped[:].rearrange("p g w t -> p (g w t)"),
            )

        last_step_of = {}
        for step, (b, c, first, width) in enumerate(pieces):
            for g in range(first // K_PASS, (first + width - 1) // K_PASS + 1):
                last_step_of[b, g] = step

        def piece_at(step):
            return pieces[step] if 0 <= step < len(pieces) else None

        def groups_at(step):
            return [group for group in sorted(last_step_of) if last_step_of[group] == step]

        def batch_at(step):
            for b, g in groups_at(step):
                if g == N_PASSES - 1:
                    return b
            return None

        x_grouped_of = {}
        x_codes_of = {}
        x_scales_of = {}
        y_ps_of = {}
        y_grouped_of = {}
        col_sum_ps_of = {}
        z_ps_of = {}
        c_ps = psum_one.tile([P, PROJ], F32)

        def regroup_x(step):
            piece = piece_at(step)
            if piece is None:
                return
            width = piece[3]
            x_grouped = stage.tile([P, width, PACK], BF16, align_bytes=64)
            x_grouped_of[piece] = x_grouped
            source = x_rows[piece][:].rearrange("p j (q i) -> p q j i", i=RUN)
            target = x_grouped[:].rearrange("p (q i) j -> p q j i", i=RUN)
            share = VECTOR_SHARE_BESIDE_Y if groups_at(step - ROUND_LAG) else VECTOR_SHARE
            split = width * share // P // RUN
            nc.vector.tensor_copy(out=target[:, :split], in_=source[:, :split])
            nc.scalar.copy(out=target[:, split:], in_=source[:, split:])

        def quantise_x(step):
            piece = piece_at(step)
            if piece is None:
                return
            b, c, first, width = piece
            if c == 0 and first == 0:
                x_codes_of[b] = codes_pool.tile(
                    [P, M_PASSES, N_COLS], U32, align_bytes=64, name="x_codes", tag="x_codes"
                )
                x_scales_of[b] = codes_pool.tile(
                    [P, M_PASSES, N_COLS], U8, align_bytes=64, name="x_scales", tag="x_scales"
                )
            cols = slice(first, first + width)
            nc.vector.quantize_mx(
                out=x_codes_of[b][:, c, cols].bitcast(FP8X4),
                scales=x_scales_of[b][:, c, cols],
                in_=x_grouped_of[piece][:].rearrange("p n j -> p (n j)"),
            )

        def project_x(step):
            piece = piece_at(step)
            if piece is None:
                return

            def operands(b, c, first):
                cols = slice(first, first + P)
                return dict(
                    lhsT=x_codes_of[b][:, c, cols].bitcast(FP8X4),
                    lhsT_scale=x_scales_of[b][:, c, cols],
                    rhs=xj_codes[:, c, :].bitcast(FP8X4),
                    rhs_scale=xj_scales[:, c, :],
                )

            for b, g in groups_at(step):
                y_ps = psum_y.tile([P, PACK, PROJ], F32)
                y_ps_of[b, g] = y_ps
                for t in range(PACK):
                    for c in range(M_PASSES):
                        nc.tensor.matmul_mx(
                            out=y_ps[:, t, :], start=(c == 0), stop=(c == M_PASSES - 1),
                            **operands(b, c, g * K_PASS + t * P),
                        )
            if step < len(FIRST_PIECES) - 1:
                return
            for b, c, first, width in pieces[0 if step < len(FIRST_PIECES) else step : step + 1]:
                if c == 0 and first == 0:
                    col_sum_ps_of[b] = psum_one.tile(
                        [P, PROJ], F32, name="col_sum_ps", tag="col_sum_ps"
                    )
                for tile_first in range(first, first + width, P):
                    nc.tensor.matmul_mx(
                        out=col_sum_ps_of[b][:],
                        start=(c == 0 and tile_first == 0),
                        stop=(batch_at(step) == b and tile_first == first + width - P),
                        **operands(b, c, tile_first),
                    )

        def round_y(step):
            groups = groups_at(step)
            if not groups:
                return
            y_grouped = stage.tile([P, len(groups), PROJ, PACK], BF16, align_bytes=64)
            y_grouped_of[step] = y_grouped
            for i, group in enumerate(groups):
                nc.scalar.copy(
                    out=y_grouped[:, i], in_=y_ps_of[group][:].rearrange("p t w -> p w t")
                )

        def add_col_sum(step, copy):
            b = batch_at(step)
            if b is None:
                return
            col_sum = finish.tile([P, PROJ], F32)
            copy(out=col_sum[:], in_=col_sum_ps_of[b][:])
            nc.tensor.matmul(
                out=c_ps[:], lhsT=select[:, b, :], rhs=col_sum[:],
                start=(b == 0), stop=(b == BATCH - 1),
            )

        def contract_y(step):
            groups = groups_at(step)
            if not groups:
                return
            y_codes = stage.tile([P, len(groups), PROJ], U32, align_bytes=64)
            y_scales = stage.tile([P, len(groups), PROJ], U8, align_bytes=64)
            nc.vector.quantize_mx(
                out=y_codes[:].rearrange("p i w -> p (i w)").bitcast(FP8X4),
                scales=y_scales[:].rearrange("p i w -> p (i w)"),
                in_=y_grouped_of[step][:].rearrange("p i w t -> p (i w t)"),
            )
            for i, (b, g) in enumerate(groups):
                if g == 0:
                    z_ps_of[b] = psum_one.tile([P, PROJ], F32, name="z_ps", tag="z_ps")
                nc.tensor.matmul_mx(
                    out=z_ps_of[b][:],
                    lhsT=xi_codes[:, g, :].bitcast(FP8X4),
                    lhsT_scale=xi_scales[:, g, :],
                    rhs=y_codes[:, i, :].bitcast(FP8X4),
                    rhs_scale=y_scales[:, i, :],
                    start=(g == 0),
                    stop=(g == N_PASSES - 1),
                )


        def statistics(what, rows, columns, count, gamma, beta, destinations):
            norm = dict(
                what=what, rows=rows, count=count, gamma=gamma, beta=beta,
                destinations=destinations, values={}, gained={},
            )
            for name in ("row_sum", "neg_mean", "row_squares", "std", "std_eps", "inverse"):
                label = what + "_" + name
                norm[name] = keep.tile([rows, columns], F32, name=label, tag=label)
            return norm

        z_norm = statistics(
            "z", P, BATCH, PROJ * PROJ, gamma_z[:], beta_z[:], [out_0[b] for b in range(BATCH)]
        )
        c_norm = statistics("c", BATCH, 1, PROJ, gamma_c[:], beta_c_plus_1[:], [out_1])
        for name in ("row_sum", "row_squares"):
            label = "z_total_" + name
            z_norm["total_" + name] = psum_one.tile([P, BATCH], F32, name=label, tag=label)
            c_norm["total_" + name] = c_norm[name]

        def add_up(norm, name, low, high):
            if norm["what"] == "z":
                nc.tensor.matmul(
                    out=norm["total_" + name][:, low:high], lhsT=ones[:],
                    rhs=norm[name][:, low:high], start=True, stop=True,
                )

        def wide_tile(norm, name):
            label = norm["what"] + "_" + name
            pool = keep if norm["what"] == "c" else finish
            return pool.tile([norm["rows"], PROJ], F32, name=label, tag=label)

        def sum_values(norm, k, values_ps):
            norm["values"][k] = wide_tile(norm, "values")
            nc.scalar.activation(
                out=norm["values"][k][:], in_=values_ps, func=ACT.Copy,
                accum_out=norm["row_sum"][:, k : k + 1],
            )
            add_up(norm, "row_sum", k, k + 1)

        def negate_means(norm, low, high):
            nc.scalar.activation(
                out=norm["neg_mean"][:, low:high], in_=norm["total_row_sum"][:, low:high],
                func=ACT.Copy, scale=-1.0 / norm["count"],
            )

        def sum_squares(norm, k):
            squares = wide_tile(norm, "squares")
            nc.scalar.activation(
                out=squares[:], in_=norm["values"][k][:], func=ACT.Square,
                bias=norm["neg_mean"][:, k : k + 1], accum_out=norm["row_squares"][:, k : k + 1],
            )

        def take_roots(norm, low, high):
            nc.scalar.activation(
                out=norm["std"][:, low:high], in_=norm["total_row_squares"][:, low:high],
                func=ACT.Sqrt, scale=1.0 / (norm["count"] - 1),
            )

        def gain(norm, k):
            norm["gained"][k] = wide_tile(norm, "gained")
            nc.vector.scalar_tensor_tensor(
                out=norm["gained"][k][:], in0=norm["values"][k][:],
                scalar=norm["neg_mean"][:, k : k + 1], in1=norm["gamma"],
                op0=ALU.add, op1=ALU.mult,
            )

        def add_eps(norm, low, high):
            nc.vector.tensor_scalar_add(
                out=norm["std_eps"][:, low:high], in0=norm["std"][:, low:high], scalar1=EPS
            )

        def invert(norm, low, high):
            nc.vector.reciprocal(
                out=norm["inverse"][:, low:high], in_=norm["std_eps"][:, low:high]
            )

        def finish_values(norm, k):
            result = wide_tile(norm, "result")
            nc.vector.scalar_tensor_tensor(
                out=result[:], in0=norm["gained"][k][:], scalar=norm["inverse"][:, k : k + 1],
                in1=norm["beta"], op0=ALU.mult, op1=ALU.add,
            )
            nc.sync.dma_start(out=norm["destinations"][k], in_=result[:])

        last = len(pieces) - 1
        final = BATCH - 1
        for step in range(last + 1):
            if step == len(FIRST_PIECES):
                prepare_small_operands()
            regroup_x(step)
            quantise_x(step - 1)
            project_x(step - 1)
            round_y(step - ROUND_LAG)
            add_col_sum(step - ROUND_LAG, nc.scalar.copy)
            contract_y(step - 3)
            b = batch_at(step - 4)
            if b is not None:
                sum_values(z_norm, b, z_ps_of[b][:])

        negate_means(z_norm, 0, final)
        for b in range(final):
            sum_squares(z_norm, b)
        quantise_x(last)
        project_x(last)
        add_up(z_norm, "row_squares", 0, final)
        gain(z_norm, 0)
        round_y(last - 1)
        contract_y(last - 1)
        gain(z_norm, 1)
        add_col_sum(last, nc.vector.tensor_copy)
        round_y(last)
        take_roots(z_norm, 0, final)
        contract_y(last)
        sum_values(z_norm, final, z_ps_of[final][:])
        add_eps(z_norm, 0, final)
        gain(z_norm, 2)
        invert(z_norm, 0, final)
        for b in range(final):
            finish_values(z_norm, b)
        sum_values(c_norm, 0, c_ps[:BATCH, :])
        negate_means(c_norm, 0, 1)
        negate_means(z_norm, final, BATCH)
        sum_squares(z_norm, final)
        add_up(z_norm, "row_squares", final, BATCH)
        sum_squares(c_norm, 0)
        take_roots(c_norm, 0, 1)
        take_roots(z_norm, final, BATCH)
        gain(z_norm, final)
        gain(c_norm, 0)
        add_eps(c_norm, 0, 1)
        add_eps(z_norm, final, BATCH)
        invert(c_norm, 0, 1)
        invert(z_norm, final, BATCH)
        finish_values(c_norm, 0)
        finish_values(z_norm, final)
